import numpy as np
import ml_dtypes


def mxq(x, axis, fmt="e4m3"):
    dtype, down = {"e4m3": (ml_dtypes.float8_e4m3fn, 7), "e5m2": (ml_dtypes.float8_e5m2, 14)}[fmt]
    v = np.moveaxis(np.asarray(x, np.float32).astype(ml_dtypes.bfloat16).astype(np.float64), axis, -1)
    blocks = v.reshape(v.shape[:-1] + (-1, 32))
    amax = np.abs(blocks).max(-1, keepdims=True)
    byte = np.maximum(np.where(amax > 0, np.frexp(amax)[1] - 1 + 127, 0) - down, 1)
    scale = np.exp2(byte - 127.0)
    codes = (blocks / scale).astype(np.float32).astype(dtype).astype(np.float64)
    return np.moveaxis((codes * scale).reshape(v.shape), -1, axis)


WIDE = False


def mx_kscale(k):
    if not WIDE:
        return np.ones(k)
    levels = np.array([10, -10, 5, -5, 0])
    a = np.random.permutation(np.resize(levels, k // 512 * 4)).reshape(k // 512, 4)
    idx = np.arange(k)
    return np.exp2(a[idx // 512, idx % 128 // 32])


BF16 = ml_dtypes.bfloat16


def bf(x):
    return np.asarray(x, np.float32).astype(BF16)


def f64(x):
    return np.asarray(x).astype(np.float64)


B, S, IN, OUT = 2, 128, 1024, 1024


def _hamilton_weight(r, i, j, k):
    col0 = np.concatenate([r, -i, -j, -k], axis=0)
    col1 = np.concatenate([i, r, -k, j], axis=0)
    col2 = np.concatenate([j, k, r, -i], axis=0)
    col3 = np.concatenate([k, -j, i, r], axis=0)
    return np.concatenate([col0, col1, col2, col3], axis=1)


def setup_inputs():
    s = mx_kscale(4 * IN)[:IN]
    sc = 1.0 / np.sqrt(2 * IN)
    return {"x": bf(np.random.standard_normal((B, S, 4 * IN)) * np.tile(s, 4)),
            "r_weight": bf(np.random.standard_normal((IN, OUT)) * sc / s[:, None]),
            "i_weight": bf(np.random.standard_normal((IN, OUT)) * sc / s[:, None]),
            "j_weight": bf(np.random.standard_normal((IN, OUT)) * sc / s[:, None]),
            "k_weight": bf(np.random.standard_normal((IN, OUT)) * sc / s[:, None]),
            "bias": bf(np.random.standard_normal(4 * OUT) * 0.5)}


def reference(x, r_weight, i_weight, j_weight, k_weight, bias):
    wq = mxq(np.concatenate([f64(r_weight), f64(i_weight), f64(j_weight), f64(k_weight)], axis=0), 0, "e4m3")
    rq, iq, jq, kq = wq[:IN], wq[IN:2 * IN], wq[2 * IN:3 * IN], wq[3 * IN:]
    W = _hamilton_weight(rq, iq, jq, kq)
    return (mxq(f64(x), 2, "e4m3") @ W) + f64(bias)

@@ -1,0 +1,227 @@
+from contextlib import ExitStack
+
+import concourse.mybir as mybir
+from concourse.masks import make_identity
+
+FP8X4 = mybir.dt.float8_e4m3fn_x4
+BF16 = mybir.dt.bfloat16
+F32 = mybir.dt.float32
+U32 = mybir.dt.uint32
+U8 = mybir.dt.uint8
+ADD = mybir.AluOpType.add
+
+P = 128
+TOKENS = 256
+IN = 1024
+OUT = 1024
+FLOPS = 2 * TOKENS * 4 * IN * 4 * OUT
+
+PIN = True
+
+NEG = ((0, 0, 0, 0), (1, 0, 0, 1), (1, 1, 0, 0), (1, 0, 1, 0))
+NEG_PLACE = {1: 0, 3: 1, 2: 2}
+
+S_COLS = (192,) + (384,) * 15
+LAST_A = 2
+LAST_B = 3
+PRE = 1
+INTER = {1: 1}
+
+
+def tile_qlinear_kernel(tc, x, r_weight, i_weight, j_weight, k_weight, bias, out):
+    nc = tc.nc
+    weights = (r_weight, i_weight, j_weight, k_weight)
+    tiles = [(w, g, h) for h in range(2) for w in range(4) for g in range(2)]
+    groups = [(m, c) for m in range(2) for c in range(4)]
+
+    with ExitStack() as ctx:
+        keep = ctx.enter_context(tc.tile_pool(name="keep", bufs=1))
+        gpool = ctx.enter_context(tc.tile_pool(name="gpool", bufs=4))
+        opool = ctx.enter_context(tc.tile_pool(name="opool", bufs=8))
+        psum = ctx.enter_context(tc.psum_pool(name="psum", bufs=1))
+        if PIN:
+            ctx.enter_context(tc.manual_schedule())
+
+        ident = keep.tile([P, P], F32, name="ident")
+        make_identity(nc, ident[:])
+
+        x_sb = [[keep.tile([P, 2048], BF16, name="x_sb%d_%d" % (m, half)) for half in range(2)] for m in range(2)]
+        for m in range(2):
+            for half in range(2):
+                nc.sync.dma_start(out=x_sb[m][half][:], in_=x[m, :, 2048 * half : 2048 * (half + 1)])
+        raw = [keep.tile([P, 4, 512], BF16, name="raw%d" % t) for t in range(16)]
+        bias_bc = keep.tile([P, 4096], BF16, name="bias_bc")
+        for t, (w, g, h) in enumerate(tiles):
+            for u in range(2):
+                r0 = 512 * g + 256 * u
+                nc.sync.dma_start(
+                    out=raw[t][:, 2 * u : 2 * u + 2, :],
+                    in_=weights[w][r0 : r0 + 256, 512 * h : 512 * (h + 1)].rearrange("(q e) c -> q e c", e=2),
+                )
+            if t == 7:
+                nc.sync.dma_start(out=bias_bc[:], in_=bias.partition_broadcast(P))
+
+        xg = [keep.tile([P, 4096], BF16, name="xg%d" % m, align_bytes=64) for m in range(2)]
+        xq = [keep.tile([P, 1024], U32, name="xq%d" % m, align_bytes=64) for m in range(2)]
+        xs = [keep.tile([P, 1024], U8, name="xs%d" % m, align_bytes=64) for m in range(2)]
+        xn = [keep.tile([P, 3072], BF16, name="xn%d" % m, align_bytes=64) for m in range(2)]
+        xnq = [keep.tile([P, 768], U32, name="xnq%d" % m, align_bytes=64) for m in range(2)]
+        xns = [keep.tile([P, 768], U8, name="xns%d" % m, align_bytes=64) for m in range(2)]
+
+        def transpose_x(m, q):
+            xw = x_sb[m][q // 2][:].bitcast(F32)
+            xgw = xg[m][:].bitcast(F32)
+            xt = psum.tile([P, 4, P], F32, name="xt%d_%d" % (m, q), tag="bank%d" % (4 * m + q))
+            for s in range(4):
+                j = 4 * (q % 2) + s
+                nc.tensor.transpose(xt[:, s, :], xw[:, P * j : P * (j + 1)], ident[:])
+            nc.scalar.copy(
+                out=xgw[:, 512 * q : 512 * (q + 1)].rearrange("p (g r u) -> p g r u", g=2, u=2),
+                in_=xt[:].rearrange("p (g u) r -> p g r u", u=2),
+            )
+
+        def quantise_x(m, half):
+            nc.vector.quantize_mx(
+                out=xq[m][:, 512 * half : 512 * (half + 1)].bitcast(FP8X4),
+                scales=xs[m][:, 512 * half : 512 * (half + 1)],
+                in_=xg[m][:, 2048 * half : 2048 * (half + 1)],
+            )
+
+        def negate_x(m, part):
+            blocks = xg[m][:].rearrange("p (b k) -> p b k", b=4)
+            if part == 0:
+                nc.vector.tensor_scalar_mul(
+                    out=xn[m][:, 0:2048].rearrange("p (b k) -> p b k", b=2), in0=blocks[:, 1:4:2, :], scalar1=-1.0
+                )
+            else:
+                nc.vector.tensor_scalar_mul(out=xn[m][:, 2048:3072], in0=xg[m][:, 2048:3072], scalar1=-1.0)
+
+        def quantise_negated_x(m, part):
+            words = slice(0, 512) if part == 0 else slice(512, 768)
+            vals = slice(0, 2048) if part == 0 else slice(2048, 3072)
+            nc.vector.quantize_mx(out=xnq[m][:, words].bitcast(FP8X4), scales=xns[m][:, words], in_=xn[m][:, vals])
+
+        wq = [keep.tile([P, 512], U32, name="wq%d" % t, align_bytes=64) for t in range(16)]
+        ws = [keep.tile([P, 512], U8, name="ws%d" % t, align_bytes=64) for t in range(16)]
+        grouped = {}
+
+        def regroup(t):
+            grp = gpool.tile([P, 512, 4], BF16, name="grp", align_bytes=64)
+            grouped[t] = grp
+            cs = S_COLS[t]
+            nc.scalar.copy(
+                out=grp[:, 0:cs, :].rearrange("p (c i) t -> p c t i", i=4),
+                in_=raw[t][:, :, 0:cs].rearrange("p t (c i) -> p c t i", i=4),
+            )
+            nc.vector.tensor_copy(
+                out=grp[:, cs:512, :].rearrange("p (c i) t -> p c t i", i=4),
+                in_=raw[t][:, :, cs:512].rearrange("p t (c i) -> p c t i", i=4),
+            )
+
+        def quantise(t):
+            nc.vector.quantize_mx(
+                out=wq[t][:].bitcast(FP8X4),
+                scales=ws[t][:],
+                in_=grouped[t][:].rearrange("p c t -> p (c t)"),
+            )
+
+        acc = {}
+
+        def open_groups():
+            for m, c in groups:
+                acc[(m, c)] = psum.tile([P, 512], F32, name="acc%d_%d" % (m, c), tag="bank%d" % (4 * m + c))
+
+        def mx_pass(t, m, c):
+            w, g, h = tiles[t]
+            b = w ^ c
+            if NEG[b][c]:
+                n = 2 * NEG_PLACE[b] + g
+                lhs, lhs_scale = xnq[m][:, P * n : P * (n + 1)], xns[m][:, P * n : P * (n + 1)]
+            else:
+                n = 2 * b + g
+                lhs, lhs_scale = xq[m][:, P * n : P * (n + 1)], xs[m][:, P * n : P * (n + 1)]
+            nc.tensor.matmul_mx(
+                out=acc[(m, c)][:],
+                lhsT=lhs.bitcast(FP8X4),
+                lhsT_scale=lhs_scale,
+                rhs=wq[t][:].bitcast(FP8X4),
+                rhs_scale=ws[t][:],
+                start=(t % 8 == 0),
+                stop=(t % 8 == 7),
+            )
+
+        def tile_major(t):
+            for m, c in groups:
+                mx_pass(t, m, c)
+
+        def finish_group(m, c, h):
+            cols = slice(1024 * c + 512 * h, 1024 * c + 512 * (h + 1))
+            o_sb = opool.tile([P, 512], F32, name="o_sb")
+            nc.vector.tensor_tensor(out=o_sb[:], in0=acc[(m, c)][:], in1=bias_bc[:, cols], op=ADD)
+            nc.sync.dma_start(out=out[m, :, cols], in_=o_sb[:])
+
+        for q in range(4):
+            transpose_x(0, q)
+            if q % 2 == 1:
+                quantise_x(0, q // 2)
+        negate_x(0, 0)
+        negate_x(0, 1)
+        transpose_x(1, 0)
+        transpose_x(1, 1)
+        regroup(0)
+        quantise(0)
+        quantise_x(1, 0)
+        transpose_x(1, 2)
+        transpose_x(1, 3)
+        quantise_x(1, 1)
+        open_groups()
+        tile_major(0)
+        quantise_negated_x(0, 0)
+        regroup(1)
+        quantise(1)
+        tile_major(1)
+        negate_x(1, 0)
+        quantise_negated_x(1, 0)
+        regroup(2)
+        quantise(2)
+        tile_major(2)
+        negate_x(1, 1)
+        quantise_negated_x(0, 1)
+        quantise_negated_x(1, 1)
+        regroup(3)
+
+        for t in range(3, 8 - LAST_A):
+            regroup(t + 1)
+            quantise(t)
+            tile_major(t)
+        for t in range(8 - LAST_A, 8):
+            regroup(t + 1)
+            quantise(t)
+        for m, c in groups:
+            for t in range(8 - LAST_A, 8):
+                mx_pass(t, m, c)
+        nxt = 8
+        for n in range(PRE):
+            regroup(nxt + 1)
+            quantise(nxt)
+            nxt += 1
+        for n, (m, c) in enumerate(groups):
+            finish_group(m, c, 0)
+            for k in range(INTER.get(n, 0)):
+                regroup(nxt + 1)
+                quantise(nxt)
+                nxt += 1
+
+        open_groups()
+        for t in range(8, nxt):
+            tile_major(t)
+        for t in range(nxt, 16):
+            if t + 1 < 16:
+                regroup(t + 1)
+            quantise(t)
+            if t < 16 - LAST_B:
+                tile_major(t)
+        for m, c in groups:
+            for t in range(16 - LAST_B, 16):
+                mx_pass(t, m, c)
+            finish_group(m, c, 1)

@@ -16,16 +16,13 @@ IN = 1024
 OUT = 1024
 FLOPS = 2 * TOKENS * 4 * IN * 4 * OUT
 
-PIN = True
+WARM = False
 
 NEG = ((0, 0, 0, 0), (1, 0, 0, 1), (1, 1, 0, 0), (1, 0, 1, 0))
-NEG_PLACE = {1: 0, 3: 1, 2: 2}
 
-S_COLS = (192,) + (384,) * 15
+S_COLS = (256, 320, 320, 320) + (384,) * 12
 LAST_A = 2
 LAST_B = 3
-PRE = 1
-INTER = {1: 1}
 
 
 def tile_qlinear_kernel(tc, x, r_weight, i_weight, j_weight, k_weight, bias, out):
@@ -39,84 +36,128 @@ def tile_qlinear_kernel(tc, x, r_weight, i_weight, j_weight, k_weight, bias, out
         gpool = ctx.enter_context(tc.tile_pool(name="gpool", bufs=4))
         opool = ctx.enter_context(tc.tile_pool(name="opool", bufs=8))
         psum = ctx.enter_context(tc.psum_pool(name="psum", bufs=1))
-        if PIN:
-            ctx.enter_context(tc.manual_schedule())
+        ctx.enter_context(tc.manual_schedule())
 
         ident = keep.tile([P, P], F32, name="ident")
         make_identity(nc, ident[:])
 
         x_sb = [[keep.tile([P, 2048], BF16, name="x_sb%d_%d" % (m, half)) for half in range(2)] for m in range(2)]
-        for m in range(2):
-            for half in range(2):
-                nc.sync.dma_start(out=x_sb[m][half][:], in_=x[m, :, 2048 * half : 2048 * (half + 1)])
         raw = [keep.tile([P, 4, 512], BF16, name="raw%d" % t) for t in range(16)]
         bias_bc = keep.tile([P, 4096], BF16, name="bias_bc")
-        for t, (w, g, h) in enumerate(tiles):
+
+        def load_x(m, half):
+            nc.sync.dma_start(out=x_sb[m][half][:], in_=x[m, :, 2048 * half : 2048 * (half + 1)])
+
+        def load_w(t):
+            w, g, h = tiles[t]
             for u in range(2):
                 r0 = 512 * g + 256 * u
                 nc.sync.dma_start(
                     out=raw[t][:, 2 * u : 2 * u + 2, :],
                     in_=weights[w][r0 : r0 + 256, 512 * h : 512 * (h + 1)].rearrange("(q e) c -> q e c", e=2),
                 )
-            if t == 7:
-                nc.sync.dma_start(out=bias_bc[:], in_=bias.partition_broadcast(P))
 
-        xg = [keep.tile([P, 4096], BF16, name="xg%d" % m, align_bytes=64) for m in range(2)]
-        xq = [keep.tile([P, 1024], U32, name="xq%d" % m, align_bytes=64) for m in range(2)]
-        xs = [keep.tile([P, 1024], U8, name="xs%d" % m, align_bytes=64) for m in range(2)]
-        xn = [keep.tile([P, 3072], BF16, name="xn%d" % m, align_bytes=64) for m in range(2)]
-        xnq = [keep.tile([P, 768], U32, name="xnq%d" % m, align_bytes=64) for m in range(2)]
-        xns = [keep.tile([P, 768], U8, name="xns%d" % m, align_bytes=64) for m in range(2)]
+        load_x(0, 0)
+        load_x(0, 1)
+        load_x(1, 0)
+        load_w(0)
+        load_x(1, 1)
+        for t in range(1, 8):
+            load_w(t)
+        nc.sync.dma_start(out=bias_bc[:], in_=bias.partition_broadcast(P))
+        for t in range(8, 16):
+            load_w(t)
+
+        warm = {}
+
+        def dummies(n, bank, rhs=None):
+            if not WARM:
+                return
+            if "zb" not in warm:
+                zb = keep.tile([P, 512], BF16, name="zb")
+                nc.vector.memset(zb[:], 0.0)
+                warm["zb"] = zb
+            scratch = psum.tile([P, 512], F32, name="scratch%d" % len(warm), tag="bank%d" % bank)
+            warm[len(warm)] = scratch
+            for k in range(n):
+                nc.tensor.matmul(
+                    out=scratch[:],
+                    lhsT=warm["zb"][:, 0:P],
+                    rhs=warm["zb"][:] if rhs is None else rhs,
+                    start=True,
+                    stop=True,
+                )
+
+        xg = keep.tile([P, 8192], BF16, name="xg", align_bytes=64)
+        xq = [keep.tile([P, 512], U32, name="xq%d" % n, align_bytes=64) for n in range(4)]
+        xs = [keep.tile([P, 512], U8, name="xs%d" % n, align_bytes=64) for n in range(4)]
+        xn = keep.tile([P, 6144], BF16, name="xn", align_bytes=64)
+        xnq = [keep.tile([P, 512], U32, name="xnq%d" % n, align_bytes=64) for n in range(3)]
+        xns = [keep.tile([P, 512], U8, name="xns%d" % n, align_bytes=64) for n in range(3)]
+        xgw = xg[:].bitcast(F32)
+        xgv = xg[:].rearrange("p (m b g k) -> p m b g k", m=2, b=4, g=2)
+        xnv = xn[:].rearrange("p (c m j k) -> p c m j k", c=3, m=2, j=2)
 
         def transpose_x(m, q):
             xw = x_sb[m][q // 2][:].bitcast(F32)
-            xgw = xg[m][:].bitcast(F32)
             xt = psum.tile([P, 4, P], F32, name="xt%d_%d" % (m, q), tag="bank%d" % (4 * m + q))
             for s in range(4):
                 j = 4 * (q % 2) + s
                 nc.tensor.transpose(xt[:, s, :], xw[:, P * j : P * (j + 1)], ident[:])
+            w0 = 2048 * m + 512 * q
             nc.scalar.copy(
-                out=xgw[:, 512 * q : 512 * (q + 1)].rearrange("p (g r u) -> p g r u", g=2, u=2),
+                out=xgw[:, w0 : w0 + 512].rearrange("p (g r u) -> p g r u", g=2, u=2),
                 in_=xt[:].rearrange("p (g u) r -> p g r u", u=2),
             )
 
         def quantise_x(m, half):
-            nc.vector.quantize_mx(
-                out=xq[m][:, 512 * half : 512 * (half + 1)].bitcast(FP8X4),
-                scales=xs[m][:, 512 * half : 512 * (half + 1)],
-                in_=xg[m][:, 2048 * half : 2048 * (half + 1)],
-            )
+            n = 2 * m + half
+            nc.vector.quantize_mx(out=xq[n][:].bitcast(FP8X4), scales=xs[n][:], in_=xg[:, 2048 * n : 2048 * (n + 1)])
 
-        def negate_x(m, part):
-            blocks = xg[m][:].rearrange("p (b k) -> p b k", b=4)
-            if part == 0:
-                nc.vector.tensor_scalar_mul(
-                    out=xn[m][:, 0:2048].rearrange("p (b k) -> p b k", b=2), in0=blocks[:, 1:4:2, :], scalar1=-1.0
-                )
+        def negate_x(m, chunks):
+            if chunks == (0, 1):
+                dst = xnv[:, 0:2, m, :, :]
+                src = xgv[:, m, 1:4:2, :, :].rearrange("p b g k -> p g b k")
+            elif chunks == (2,):
+                dst = xnv[:, 2, m, :, :]
+                src = xgv[:, m, 2, :, :]
             else:
-                nc.vector.tensor_scalar_mul(out=xn[m][:, 2048:3072], in0=xg[m][:, 2048:3072], scalar1=-1.0)
+                dst = xnv[:, chunks[0], m, :, :]
+                src = xgv[:, m, 1:4:2, chunks[0], :]
+            nc.vector.tensor_scalar_mul(out=dst, in0=src, scalar1=-1.0)
 
-        def quantise_negated_x(m, part):
-            words = slice(0, 512) if part == 0 else slice(512, 768)
-            vals = slice(0, 2048) if part == 0 else slice(2048, 3072)
-            nc.vector.quantize_mx(out=xnq[m][:, words].bitcast(FP8X4), scales=xns[m][:, words], in_=xn[m][:, vals])
+        def quantise_negated_x(chunk):
+            nc.vector.quantize_mx(
+                out=xnq[chunk][:].bitcast(FP8X4), scales=xns[chunk][:], in_=xn[:, 2048 * chunk : 2048 * (chunk + 1)]
+            )
 
         wq = [keep.tile([P, 512], U32, name="wq%d" % t, align_bytes=64) for t in range(16)]
         ws = [keep.tile([P, 512], U8, name="ws%d" % t, align_bytes=64) for t in range(16)]
         grouped = {}
 
-        def regroup(t):
-            grp = gpool.tile([P, 512, 4], BF16, name="grp", align_bytes=64)
-            grouped[t] = grp
+        def grouped_tile(t):
+            if t not in grouped:
+                grp = gpool.tile([P, 512, 4], BF16, name="grp", align_bytes=64)
+                grouped[t] = grp
+            return grouped[t]
+
+        def regroup_s(t):
             cs = S_COLS[t]
             nc.scalar.copy(
-                out=grp[:, 0:cs, :].rearrange("p (c i) t -> p c t i", i=4),
+                out=grouped_tile(t)[:, 0:cs, :].rearrange("p (c i) t -> p c t i", i=4),
                 in_=raw[t][:, :, 0:cs].rearrange("p t (c i) -> p c t i", i=4),
             )
+
+        def regroup_v(t):
+            cs = S_COLS[t]
             nc.vector.tensor_copy(
-                out=grp[:, cs:512, :].rearrange("p (c i) t -> p c t i", i=4),
+                out=grouped_tile(t)[:, cs:512, :].rearrange("p (c i) t -> p c t i", i=4),
                 in_=raw[t][:, :, cs:512].rearrange("p t (c i) -> p c t i", i=4),
             )
+
+        def regroup(t):
+            regroup_s(t)
+            regroup_v(t)
 
         def quantise(t):
             nc.vector.quantize_mx(
@@ -127,101 +168,118 @@ def tile_qlinear_kernel(tc, x, r_weight, i_weight, j_weight, k_weight, bias, out
 
         acc = {}
 
-        def open_groups():
-            for m, c in groups:
-                acc[(m, c)] = psum.tile([P, 512], F32, name="acc%d_%d" % (m, c), tag="bank%d" % (4 * m + c))
+        def open_group(m, c):
+            acc[(m, c)] = psum.tile([P, 512], F32, name="acc%d_%d" % (m, c), tag="bank%d" % (4 * m + c))
 
-        def mx_pass(t, m, c):
+        def mx_pass(t, m, c, dst, cols):
             w, g, h = tiles[t]
             b = w ^ c
             if NEG[b][c]:
-                n = 2 * NEG_PLACE[b] + g
-                lhs, lhs_scale = xnq[m][:, P * n : P * (n + 1)], xns[m][:, P * n : P * (n + 1)]
+                chunk, j = (2, g) if b == 2 else (g, (b - 1) // 2)
+                n = 2 * m + j
+                lhs, lhs_scale = xnq[chunk][:, P * n : P * (n + 1)], xns[chunk][:, P * n : P * (n + 1)]
             else:
-                n = 2 * b + g
-                lhs, lhs_scale = xq[m][:, P * n : P * (n + 1)], xs[m][:, P * n : P * (n + 1)]
+                n = 2 * (b % 2) + g
+                lhs, lhs_scale = xq[2 * m + b // 2][:, P * n : P * (n + 1)], xs[2 * m + b // 2][:, P * n : P * (n + 1)]
             nc.tensor.matmul_mx(
-                out=acc[(m, c)][:],
+                out=dst,
                 lhsT=lhs.bitcast(FP8X4),
                 lhsT_scale=lhs_scale,
-                rhs=wq[t][:].bitcast(FP8X4),
-                rhs_scale=ws[t][:],
+                rhs=wq[t][:, cols].bitcast(FP8X4),
+                rhs_scale=ws[t][:, cols],
                 start=(t % 8 == 0),
                 stop=(t % 8 == 7),
             )
 
-        def tile_major(t):
-            for m, c in groups:
-                mx_pass(t, m, c)
+        def full_pass(t, m, c):
+            mx_pass(t, m, c, acc[(m, c)][:], slice(0, 512))
+
+        def finish(src, m, col0, width):
+            o_sb = opool.tile([P, 512], F32, name="o_sb")
+            nc.vector.tensor_tensor(out=o_sb[:, 0:width], in0=src, in1=bias_bc[:, col0 : col0 + width], op=ADD)
+            nc.sync.dma_start(out=out[m, :, col0 : col0 + width], in_=o_sb[:, 0:width])
 
         def finish_group(m, c, h):
-            cols = slice(1024 * c + 512 * h, 1024 * c + 512 * (h + 1))
-            o_sb = opool.tile([P, 512], F32, name="o_sb")
-            nc.vector.tensor_tensor(out=o_sb[:], in0=acc[(m, c)][:], in1=bias_bc[:, cols], op=ADD)
-            nc.sync.dma_start(out=out[m, :, cols], in_=o_sb[:])
+            finish(acc[(m, c)][:], m, 1024 * c + 512 * h, 512)
 
-        for q in range(4):
-            transpose_x(0, q)
-            if q % 2 == 1:
-                quantise_x(0, q // 2)
-        negate_x(0, 0)
-        negate_x(0, 1)
+        dummies(8, 7)
+        transpose_x(0, 0)
+        transpose_x(0, 1)
+        quantise_x(0, 0)
+        dummies(1, 7)
+        transpose_x(0, 2)
+        negate_x(0, (2,))
+        transpose_x(0, 3)
+        quantise_x(0, 1)
+        dummies(1, 7)
         transpose_x(1, 0)
-        transpose_x(1, 1)
         regroup(0)
+        negate_x(0, (0, 1))
         quantise(0)
+        transpose_x(1, 1)
         quantise_x(1, 0)
+        dummies(3, 7, raw[0][:, 0, :])
+        regroup_v(1)
         transpose_x(1, 2)
+        negate_x(1, (2,))
         transpose_x(1, 3)
         quantise_x(1, 1)
-        open_groups()
-        tile_major(0)
-        quantise_negated_x(0, 0)
-        regroup(1)
+        for m, c in groups:
+            open_group(m, c)
+        for m, c in groups:
+            full_pass(0, m, c)
+        regroup_s(1)
+        negate_x(1, (0,))
+        quantise_negated_x(0)
         quantise(1)
-        tile_major(1)
-        negate_x(1, 0)
-        quantise_negated_x(1, 0)
+        for m, c in groups:
+            full_pass(1, m, c)
         regroup(2)
         quantise(2)
-        tile_major(2)
-        negate_x(1, 1)
-        quantise_negated_x(0, 1)
-        quantise_negated_x(1, 1)
+        for m, c in groups:
+            full_pass(2, m, c)
+        negate_x(1, (1,))
+        quantise_negated_x(1)
         regroup(3)
+        quantise(3)
+        for m, c in groups:
+            full_pass(3, m, c)
+        quantise_negated_x(2)
+        regroup(4)
 
-        for t in range(3, 8 - LAST_A):
+        for t in range(4, 8):
             regroup(t + 1)
             quantise(t)
-            tile_major(t)
-        for t in range(8 - LAST_A, 8):
-            regroup(t + 1)
-            quantise(t)
+            if t < 8 - LAST_A:
+                for m, c in groups:
+                    full_pass(t, m, c)
         for m, c in groups:
             for t in range(8 - LAST_A, 8):
-                mx_pass(t, m, c)
-        nxt = 8
-        for n in range(PRE):
-            regroup(nxt + 1)
-            quantise(nxt)
-            nxt += 1
-        for n, (m, c) in enumerate(groups):
-            finish_group(m, c, 0)
-            for k in range(INTER.get(n, 0)):
-                regroup(nxt + 1)
-                quantise(nxt)
-                nxt += 1
-
-        open_groups()
-        for t in range(8, nxt):
-            tile_major(t)
-        for t in range(nxt, 16):
-            if t + 1 < 16:
-                regroup(t + 1)
-            quantise(t)
-            if t < 16 - LAST_B:
-                tile_major(t)
+                full_pass(t, m, c)
+        regroup(9)
+        quantise(8)
+        regroup(10)
         for m, c in groups:
+            finish_group(m, c, 0)
+
+        early = groups[:7]
+        for m, c in early:
+            open_group(m, c)
+        for t in range(8, 16):
+            if t > 8:
+                quantise(t)
+            if 11 <= t + 2 < 16:
+                regroup(t + 2)
+            if t < 16 - LAST_B:
+                for m, c in early:
+                    full_pass(t, m, c)
+        for m, c in early:
             for t in range(16 - LAST_B, 16):
-                mx_pass(t, m, c)
+                full_pass(t, m, c)
             finish_group(m, c, 1)
+        m, c = groups[7]
+        for half, bank in ((0, 7), (1, 0)):
+            part = psum.tile([P, 256], F32, name="part%d" % half, tag="bank%d" % bank)
+            for t in range(8, 16):
+                mx_pass(t, m, c, part[:], slice(256 * half, 256 * (half + 1)))
+            finish(part[:], m, 1024 * c + 512 + 256 * half, 256)

@@ -16,7 +16,7 @@ IN = 1024
 OUT = 1024
 FLOPS = 2 * TOKENS * 4 * IN * 4 * OUT
 
-WARM = False
+WARM = True
 
 NEG = ((0, 0, 0, 0), (1, 0, 0, 1), (1, 1, 0, 0), (1, 0, 1, 0))
 
@@ -204,11 +204,13 @@ def tile_qlinear_kernel(tc, x, r_weight, i_weight, j_weight, k_weight, bias, out
 
         dummies(8, 7)
         transpose_x(0, 0)
+        dummies(1, 7)
         transpose_x(0, 1)
         quantise_x(0, 0)
         dummies(1, 7)
         transpose_x(0, 2)
         negate_x(0, (2,))
+        dummies(1, 7)
         transpose_x(0, 3)
         quantise_x(0, 1)
         dummies(1, 7)
@@ -216,12 +218,15 @@ def tile_qlinear_kernel(tc, x, r_weight, i_weight, j_weight, k_weight, bias, out
         regroup(0)
         negate_x(0, (0, 1))
         quantise(0)
+        dummies(1, 7)
         transpose_x(1, 1)
         quantise_x(1, 0)
+        dummies(1, 7)
         dummies(3, 7, raw[0][:, 0, :])
         regroup_v(1)
         transpose_x(1, 2)
         negate_x(1, (2,))
+        dummies(1, 7)
         transpose_x(1, 3)
         quantise_x(1, 1)
         for m, c in groups:

@@ -20,7 +20,7 @@ WARM = True
 
 NEG = ((0, 0, 0, 0), (1, 0, 0, 1), (1, 1, 0, 0), (1, 0, 1, 0))
 
-S_COLS = (256, 320, 320, 320) + (384,) * 12
+S_COLS = (256, 192, 320, 320) + (384,) * 12
 LAST_A = 2
 LAST_B = 3
 
@@ -204,29 +204,25 @@ def tile_qlinear_kernel(tc, x, r_weight, i_weight, j_weight, k_weight, bias, out
 
         dummies(8, 7)
         transpose_x(0, 0)
-        dummies(1, 7)
         transpose_x(0, 1)
         quantise_x(0, 0)
         dummies(1, 7)
         transpose_x(0, 2)
         negate_x(0, (2,))
-        dummies(1, 7)
         transpose_x(0, 3)
         quantise_x(0, 1)
         dummies(1, 7)
-        transpose_x(1, 0)
-        regroup(0)
         negate_x(0, (0, 1))
-        quantise(0)
-        dummies(1, 7)
+        transpose_x(1, 0)
         transpose_x(1, 1)
-        quantise_x(1, 0)
         dummies(1, 7)
-        dummies(3, 7, raw[0][:, 0, :])
-        regroup_v(1)
+        regroup(0)
+        quantise_x(1, 0)
+        quantise(0)
+        dummies(2, 7, raw[0][:, 0, :])
         transpose_x(1, 2)
         negate_x(1, (2,))
-        dummies(1, 7)
+        regroup_v(1)
         transpose_x(1, 3)
         quantise_x(1, 1)
         for m, c in groups:
@@ -234,11 +230,11 @@ def tile_qlinear_kernel(tc, x, r_weight, i_weight, j_weight, k_weight, bias, out
         for m, c in groups:
             full_pass(0, m, c)
         regroup_s(1)
-        negate_x(1, (0,))
-        quantise_negated_x(0)
         quantise(1)
         for m, c in groups:
             full_pass(1, m, c)
+        negate_x(1, (0,))
+        quantise_negated_x(0)
         regroup(2)
         quantise(2)
         for m, c in groups:

@@ -22,7 +22,7 @@ NEG = ((0, 0, 0, 0), (1, 0, 0, 1), (1, 1, 0, 0), (1, 0, 1, 0))
 
 S_COLS = (256, 192, 320, 320) + (384,) * 12
 LAST_A = 2
-LAST_B = 3
+LAST_B = 2
 
 
 def tile_qlinear_kernel(tc, x, r_weight, i_weight, j_weight, k_weight, bias, out):
@@ -62,10 +62,10 @@ def tile_qlinear_kernel(tc, x, r_weight, i_weight, j_weight, k_weight, bias, out
         load_x(1, 0)
         load_w(0)
         load_x(1, 1)
-        for t in range(1, 8):
+        for t in range(1, 9):
             load_w(t)
         nc.sync.dma_start(out=bias_bc[:], in_=bias.partition_broadcast(P))
-        for t in range(8, 16):
+        for t in range(9, 16):
             load_w(t)
 
         warm = {}
@@ -257,20 +257,23 @@ def tile_qlinear_kernel(tc, x, r_weight, i_weight, j_weight, k_weight, bias, out
         for m, c in groups:
             for t in range(8 - LAST_A, 8):
                 full_pass(t, m, c)
-        regroup(9)
         quantise(8)
-        regroup(10)
-        for m, c in groups:
+        regroup_s(9)
+        for n, (m, c) in enumerate(groups):
+            if n == 5:
+                regroup_v(9)
+                quantise(9)
             finish_group(m, c, 0)
+        regroup(10)
 
         early = groups[:7]
         for m, c in early:
             open_group(m, c)
         for t in range(8, 16):
-            if t > 8:
+            if t > 9:
+                if t + 1 < 16:
+                    regroup(t + 1)
                 quantise(t)
-            if 11 <= t + 2 < 16:
-                regroup(t + 2)
             if t < 16 - LAST_B:
                 for m, c in early:
                     full_pass(t, m, c)

@@ -16,13 +16,13 @@ IN = 1024
 OUT = 1024
 FLOPS = 2 * TOKENS * 4 * IN * 4 * OUT
 
-WARM = True
+WARM = False
 
 NEG = ((0, 0, 0, 0), (1, 0, 0, 1), (1, 1, 0, 0), (1, 0, 1, 0))
 
 S_COLS = (256, 192, 320, 320) + (384,) * 12
 LAST_A = 2
-LAST_B = 2
+LAST_B = 3
 
 
 def tile_qlinear_kernel(tc, x, r_weight, i_weight, j_weight, k_weight, bias, out):
@@ -62,10 +62,10 @@ def tile_qlinear_kernel(tc, x, r_weight, i_weight, j_weight, k_weight, bias, out
         load_x(1, 0)
         load_w(0)
         load_x(1, 1)
-        for t in range(1, 9):
+        for t in range(1, 8):
             load_w(t)
         nc.sync.dma_start(out=bias_bc[:], in_=bias.partition_broadcast(P))
-        for t in range(9, 16):
+        for t in range(8, 16):
             load_w(t)
 
         warm = {}
@@ -257,23 +257,20 @@ def tile_qlinear_kernel(tc, x, r_weight, i_weight, j_weight, k_weight, bias, out
         for m, c in groups:
             for t in range(8 - LAST_A, 8):
                 full_pass(t, m, c)
+        regroup(9)
         quantise(8)
-        regroup_s(9)
-        for n, (m, c) in enumerate(groups):
-            if n == 5:
-                regroup_v(9)
-                quantise(9)
-            finish_group(m, c, 0)
         regroup(10)
+        for m, c in groups:
+            finish_group(m, c, 0)
 
         early = groups[:7]
         for m, c in early:
             open_group(m, c)
         for t in range(8, 16):
-            if t > 9:
-                if t + 1 < 16:
-                    regroup(t + 1)
+            if t > 8:
                 quantise(t)
+            if 11 <= t + 2 < 16:
+                regroup(t + 2)
             if t < 16 - LAST_B:
                 for m, c in early:
                     full_pass(t, m, c)

@@ -16,7 +16,7 @@ IN = 1024
 OUT = 1024
 FLOPS = 2 * TOKENS * 4 * IN * 4 * OUT
 
-WARM = False
+WARM = True
 
 NEG = ((0, 0, 0, 0), (1, 0, 0, 1), (1, 1, 0, 0), (1, 0, 1, 0))
 
@@ -219,12 +219,13 @@ def tile_qlinear_kernel(tc, x, r_weight, i_weight, j_weight, k_weight, bias, out
         regroup(0)
         quantise_x(1, 0)
         quantise(0)
-        dummies(2, 7, raw[0][:, 0, :])
+        dummies(4, 7, raw[0][:, 0, :])
         transpose_x(1, 2)
         negate_x(1, (2,))
         regroup_v(1)
         transpose_x(1, 3)
         quantise_x(1, 1)
+        dummies(2, 0)
         for m, c in groups:
             open_group(m, c)
         for m, c in groups:

from contextlib import ExitStack

import concourse.mybir as mybir
from concourse.masks import make_identity

FP8X4 = mybir.dt.float8_e4m3fn_x4
BF16 = mybir.dt.bfloat16
F32 = mybir.dt.float32
U32 = mybir.dt.uint32
U8 = mybir.dt.uint8
ADD = mybir.AluOpType.add

P = 128
TOKENS = 256
IN = 1024
OUT = 1024
FLOPS = 2 * TOKENS * 4 * IN * 4 * OUT

WARM = True

NEG = ((0, 0, 0, 0), (1, 0, 0, 1), (1, 1, 0, 0), (1, 0, 1, 0))

S_COLS = (256, 192, 320, 320) + (384,) * 12
LAST_A = 2
LAST_B = 3


def tile_qlinear_kernel(tc, x, r_weight, i_weight, j_weight, k_weight, bias, out):
    nc = tc.nc
    weights = (r_weight, i_weight, j_weight, k_weight)
    tiles = [(w, g, h) for h in range(2) for w in range(4) for g in range(2)]
    groups = [(m, c) for m in range(2) for c in range(4)]

    with ExitStack() as ctx:
        keep = ctx.enter_context(tc.tile_pool(name="keep", bufs=1))
        gpool = ctx.enter_context(tc.tile_pool(name="gpool", bufs=4))
        opool = ctx.enter_context(tc.tile_pool(name="opool", bufs=8))
        psum = ctx.enter_context(tc.psum_pool(name="psum", bufs=1))
        ctx.enter_context(tc.manual_schedule())

        ident = keep.tile([P, P], F32, name="ident")
        make_identity(nc, ident[:])

        x_sb = [[keep.tile([P, 2048], BF16, name="x_sb%d_%d" % (m, half)) for half in range(2)] for m in range(2)]
        raw = [keep.tile([P, 4, 512], BF16, name="raw%d" % t) for t in range(16)]
        bias_bc = keep.tile([P, 4096], BF16, name="bias_bc")

        def load_x(m, half):
            nc.sync.dma_start(out=x_sb[m][half][:], in_=x[m, :, 2048 * half : 2048 * (half + 1)])

        def load_w(t):
            w, g, h = tiles[t]
            for u in range(2):
                r0 = 512 * g + 256 * u
                nc.sync.dma_start(
                    out=raw[t][:, 2 * u : 2 * u + 2, :],
                    in_=weights[w][r0 : r0 + 256, 512 * h : 512 * (h + 1)].rearrange("(q e) c -> q e c", e=2),
                )

        load_x(0, 0)
        load_x(0, 1)
        load_x(1, 0)
        load_w(0)
        load_x(1, 1)
        for t in range(1, 8):
            load_w(t)
        nc.sync.dma_start(out=bias_bc[:], in_=bias.partition_broadcast(P))
        for t in range(8, 16):
            load_w(t)

        warm = {}

        def dummies(n, bank, rhs=None):
            if not WARM:
                return
            if "zb" not in warm:
                zb = keep.tile([P, 512], BF16, name="zb")
                nc.vector.memset(zb[:], 0.0)
                warm["zb"] = zb
            scratch = psum.tile([P, 512], F32, name="scratch%d" % len(warm), tag="bank%d" % bank)
            warm[len(warm)] = scratch
            for k in range(n):
                nc.tensor.matmul(
                    out=scratch[:],
                    lhsT=warm["zb"][:, 0:P],
                    rhs=warm["zb"][:] if rhs is None else rhs,
                    start=True,
                    stop=True,
                )

        xg = keep.tile([P, 8192], BF16, name="xg", align_bytes=64)
        xq = [keep.tile([P, 512], U32, name="xq%d" % n, align_bytes=64) for n in range(4)]
        xs = [keep.tile([P, 512], U8, name="xs%d" % n, align_bytes=64) for n in range(4)]
        xn = keep.tile([P, 6144], BF16, name="xn", align_bytes=64)
        xnq = [keep.tile([P, 512], U32, name="xnq%d" % n, align_bytes=64) for n in range(3)]
        xns = [keep.tile([P, 512], U8, name="xns%d" % n, align_bytes=64) for n in range(3)]
        xgw = xg[:].bitcast(F32)
        xgv = xg[:].rearrange("p (m b g k) -> p m b g k", m=2, b=4, g=2)
        xnv = xn[:].rearrange("p (c m j k) -> p c m j k", c=3, m=2, j=2)

        def transpose_x(m, q):
            xw = x_sb[m][q // 2][:].bitcast(F32)
            xt = psum.tile([P, 4, P], F32, name="xt%d_%d" % (m, q), tag="bank%d" % (4 * m + q))
            for s in range(4):
                j = 4 * (q % 2) + s
                nc.tensor.transpose(xt[:, s, :], xw[:, P * j : P * (j + 1)], ident[:])
            w0 = 2048 * m + 512 * q
            nc.scalar.copy(
                out=xgw[:, w0 : w0 + 512].rearrange("p (g r u) -> p g r u", g=2, u=2),
                in_=xt[:].rearrange("p (g u) r -> p g r u", u=2),
            )

        def quantise_x(m, half):
            n = 2 * m + half
            nc.vector.quantize_mx(out=xq[n][:].bitcast(FP8X4), scales=xs[n][:], in_=xg[:, 2048 * n : 2048 * (n + 1)])

        def negate_x(m, chunks):
            if chunks == (0, 1):
                dst = xnv[:, 0:2, m, :, :]
                src = xgv[:, m, 1:4:2, :, :].rearrange("p b g k -> p g b k")
            elif chunks == (2,):
                dst = xnv[:, 2, m, :, :]
                src = xgv[:, m, 2, :, :]
            else:
                dst = xnv[:, chunks[0], m, :, :]
                src = xgv[:, m, 1:4:2, chunks[0], :]
            nc.vector.tensor_scalar_mul(out=dst, in0=src, scalar1=-1.0)

        def quantise_negated_x(chunk):
            nc.vector.quantize_mx(
                out=xnq[chunk][:].bitcast(FP8X4), scales=xns[chunk][:], in_=xn[:, 2048 * chunk : 2048 * (chunk + 1)]
            )

        wq = [keep.tile([P, 512], U32, name="wq%d" % t, align_bytes=64) for t in range(16)]
        ws = [keep.tile([P, 512], U8, name="ws%d" % t, align_bytes=64) for t in range(16)]
        grouped = {}

        def grouped_tile(t):
            if t not in grouped:
                grp = gpool.tile([P, 512, 4], BF16, name="grp", align_bytes=64)
                grouped[t] = grp
            return grouped[t]

        def regroup_s(t):
            cs = S_COLS[t]
            nc.scalar.copy(
                out=grouped_tile(t)[:, 0:cs, :].rearrange("p (c i) t -> p c t i", i=4),
                in_=raw[t][:, :, 0:cs].rearrange("p t (c i) -> p c t i", i=4),
            )

        def regroup_v(t):
            cs = S_COLS[t]
            nc.vector.tensor_copy(
                out=grouped_tile(t)[:, cs:512, :].rearrange("p (c i) t -> p c t i", i=4),
                in_=raw[t][:, :, cs:512].rearrange("p t (c i) -> p c t i", i=4),
            )

        def regroup(t):
            regroup_s(t)
            regroup_v(t)

        def quantise(t):
            nc.vector.quantize_mx(
                out=wq[t][:].bitcast(FP8X4),
                scales=ws[t][:],
                in_=grouped[t][:].rearrange("p c t -> p (c t)"),
            )

        acc = {}

        def open_group(m, c):
            acc[(m, c)] = psum.tile([P, 512], F32, name="acc%d_%d" % (m, c), tag="bank%d" % (4 * m + c))

        def mx_pass(t, m, c, dst, cols):
            w, g, h = tiles[t]
            b = w ^ c
            if NEG[b][c]:
                chunk, j = (2, g) if b == 2 else (g, (b - 1) // 2)
                n = 2 * m + j
                lhs, lhs_scale = xnq[chunk][:, P * n : P * (n + 1)], xns[chunk][:, P * n : P * (n + 1)]
            else:
                n = 2 * (b % 2) + g
                lhs, lhs_scale = xq[2 * m + b // 2][:, P * n : P * (n + 1)], xs[2 * m + b // 2][:, P * n : P * (n + 1)]
            nc.tensor.matmul_mx(
                out=dst,
                lhsT=lhs.bitcast(FP8X4),
                lhsT_scale=lhs_scale,
                rhs=wq[t][:, cols].bitcast(FP8X4),
                rhs_scale=ws[t][:, cols],
                start=(t % 8 == 0),
                stop=(t % 8 == 7),
            )

        def full_pass(t, m, c):
            mx_pass(t, m, c, acc[(m, c)][:], slice(0, 512))

        def finish(src, m, col0, width):
            o_sb = opool.tile([P, 512], F32, name="o_sb")
            nc.vector.tensor_tensor(out=o_sb[:, 0:width], in0=src, in1=bias_bc[:, col0 : col0 + width], op=ADD)
            nc.sync.dma_start(out=out[m, :, col0 : col0 + width], in_=o_sb[:, 0:width])

        def finish_group(m, c, h):
            finish(acc[(m, c)][:], m, 1024 * c + 512 * h, 512)

        dummies(8, 7)
        transpose_x(0, 0)
        transpose_x(0, 1)
        quantise_x(0, 0)
        dummies(1, 7)
        transpose_x(0, 2)
        negate_x(0, (2,))
        transpose_x(0, 3)
        quantise_x(0, 1)
        dummies(1, 7)
        negate_x(0, (0, 1))
        transpose_x(1, 0)
        transpose_x(1, 1)
        dummies(1, 7)
        regroup(0)
        quantise_x(1, 0)
        quantise(0)
        dummies(4, 7, raw[0][:, 0, :])
        transpose_x(1, 2)
        negate_x(1, (2,))
        regroup_v(1)
        transpose_x(1, 3)
        quantise_x(1, 1)
        dummies(2, 0)
        for m, c in groups:
            open_group(m, c)
        for m, c in groups:
            full_pass(0, m, c)
        regroup_s(1)
        quantise(1)
        for m, c in groups:
            full_pass(1, m, c)
        negate_x(1, (0,))
        quantise_negated_x(0)
        regroup(2)
        quantise(2)
        for m, c in groups:
            full_pass(2, m, c)
        negate_x(1, (1,))
        quantise_negated_x(1)
        regroup(3)
        quantise(3)
        for m, c in groups:
            full_pass(3, m, c)
        quantise_negated_x(2)
        regroup(4)

        for t in range(4, 8):
            regroup(t + 1)
            quantise(t)
            if t < 8 - LAST_A:
                for m, c in groups:
                    full_pass(t, m, c)
        for m, c in groups:
            for t in range(8 - LAST_A, 8):
                full_pass(t, m, c)
        regroup(9)
        quantise(8)
        regroup(10)
        for m, c in groups:
            finish_group(m, c, 0)

        early = groups[:7]
        for m, c in early:
            open_group(m, c)
        for t in range(8, 16):
            if t > 8:
                quantise(t)
            if 11 <= t + 2 < 16:
                regroup(t + 2)
            if t < 16 - LAST_B:
                for m, c in early:
                    full_pass(t, m, c)
        for m, c in early:
            for t in range(16 - LAST_B, 16):
                full_pass(t, m, c)
            finish_group(m, c, 1)
        m, c = groups[7]
        for half, bank in ((0, 7), (1, 0)):
            part = psum.tile([P, 256], F32, name="part%d" % half, tag="bank%d" % bank)
            for t in range(8, 16):
                mx_pass(t, m, c, part[:], slice(256 * half, 256 * (half + 1)))
            finish(part[:], m, 1024 * c + 512 + 256 * half, 256)
